import numpy as np
import ml_dtypes


def mxq(x, axis, fmt="e4m3"):
    dtype, down = {"e4m3": (ml_dtypes.float8_e4m3fn, 7), "e5m2": (ml_dtypes.float8_e5m2, 14)}[fmt]
    v = np.moveaxis(np.asarray(x, np.float32).astype(ml_dtypes.bfloat16).astype(np.float64), axis, -1)
    blocks = v.reshape(v.shape[:-1] + (-1, 32))
    amax = np.abs(blocks).max(-1, keepdims=True)
    byte = np.maximum(np.where(amax > 0, np.frexp(amax)[1] - 1 + 127, 0) - down, 1)
    scale = np.exp2(byte - 127.0)
    codes = (blocks / scale).astype(np.float32).astype(dtype).astype(np.float64)
    return np.moveaxis((codes * scale).reshape(v.shape), -1, axis)


WIDE = False


def mx_kscale(k):
    if not WIDE:
        return np.ones(k)
    levels = np.array([10, -10, 5, -5, 0])
    a = np.random.permutation(np.resize(levels, k // 512 * 4)).reshape(k // 512, 4)
    idx = np.arange(k)
    return np.exp2(a[idx // 512, idx % 128 // 32])


BF16 = ml_dtypes.bfloat16


def bf(x):
    return np.asarray(x, np.float32).astype(BF16)


def f64(x):
    return np.asarray(x).astype(np.float64)


B, S, D, H, DH = 4, 2048, 1024, 1, 64
ROPE_BASE = 10000.0


def rope_tables():
    inv_freq = 1.0 / (ROPE_BASE ** (f64(np.arange(0, DH, 2)) / DH))
    freqs = f64(np.arange(S))[:, None] * inv_freq[None, :]
    return np.cos(freqs), np.sin(freqs)


def rope_interleaved(t, cos, sin):
    x1 = t[..., 0::2]
    x2 = t[..., 1::2]
    c = cos[None, :, None, :]
    s_ = sin[None, :, None, :]
    even = x1 * c - x2 * s_
    odd = x1 * s_ + x2 * c
    return np.stack((even, odd), axis=-1).reshape(t.shape)


def setup_inputs():
    s = mx_kscale(D)
    return {"x": bf(np.random.standard_normal((B, S, D)) * s),
            "wqk_w": bf(np.random.standard_normal((2 * H * DH, D)) / np.sqrt(D) / s[None, :])}


def reference(x, wqk_w):
    xqk = (mxq(f64(x), 2, "e4m3") @ mxq(f64(wqk_w), 1, "e4m3").T).reshape(B, S, 2, H, DH)
    cos, sin = rope_tables()
    q = rope_interleaved(xqk[:, :, 0], cos, sin).transpose(0, 2, 1, 3)
    k = rope_interleaved(xqk[:, :, 1], cos, sin).transpose(0, 2, 1, 3)
    return q, k

@@ -1,0 +1,232 @@
+import math
+from contextlib import ExitStack
+
+import concourse.mybir as mybir
+from concourse.masks import make_identity
+
+F32 = mybir.dt.float32
+BF16 = mybir.dt.bfloat16
+I32 = mybir.dt.int32
+U32 = mybir.dt.uint32
+U8 = mybir.dt.uint8
+FP8X4 = mybir.dt.float8_e4m3fn_x4
+ALU = mybir.AluOpType
+ACT = mybir.ActivationFunctionType
+
+P = 128
+BATCH, SEQ, D_IN = 4, 2048, 1024
+HEAD = 64
+PAIRS = HEAD // 2
+D_OUT = 2 * HEAD
+ROPE_BASE = 10000.0
+
+K_PASS = 4 * P
+PASSES = D_IN // K_PASS
+WORDS = D_IN // 2
+
+POS_PER_PART = SEQ // P
+ROUND_TILES = 4
+ROUNDS_PER_BATCH = POS_PER_PART // ROUND_TILES
+ROUNDS = BATCH * ROUNDS_PER_BATCH
+ROUND_OUT = ROUND_TILES * D_OUT
+LOADS_AHEAD = 6
+
+ROUND_MAGIC = 1.5 * 2.0**23
+
+FLOPS = 2 * BATCH * SEQ * D_IN * D_OUT
+
+
+def turns_per_position(i):
+    return 1.0 / (ROPE_BASE ** (2.0 * i / HEAD) * 2.0 * math.pi)
+
+
+def tile_attention_pa_t_kernel(tc, x, wqk_w, out_0, out_1):
+    nc = tc.nc
+    with ExitStack() as ctx:
+        const = ctx.enter_context(tc.tile_pool(name="const", bufs=1))
+        row_pool = ctx.enter_context(tc.tile_pool(name="rows", bufs=LOADS_AHEAD + 2))
+        mx_pool = ctx.enter_context(tc.tile_pool(name="mx_operands", bufs=3))
+        rope_pool = ctx.enter_context(tc.tile_pool(name="rope", bufs=2))
+        out_pool = ctx.enter_context(tc.tile_pool(name="rotated", bufs=4))
+        flip_banks = ctx.enter_context(tc.psum_pool(name="flip_banks", bufs=6))
+        sum_banks = ctx.enter_context(tc.psum_pool(name="sum_banks", bufs=2))
+        ctx.enter_context(tc.manual_schedule())
+
+        x_runs = x.rearrange("b (p t) d -> b p (t d)", t=POS_PER_PART)
+        out_runs = [
+            out.rearrange("b h (p t) f -> (b h) p (t f)", t=POS_PER_PART) for out in (out_0, out_1)
+        ]
+
+        def load_round(r):
+            batch, part = divmod(r, ROUNDS_PER_BATCH)
+            rows = row_pool.tile([P, ROUND_TILES * D_IN], BF16)
+            nc.sync.dma_start(
+                out=rows[:],
+                in_=x_runs[batch, :, part * ROUND_TILES * D_IN : (part + 1) * ROUND_TILES * D_IN],
+            )
+            return rows
+
+        def k_onto_partitions(row_words, grouped_words):
+            bank = flip_banks.tile([P, WORDS], F32)
+            for q in range(WORDS // P):
+                nc.tensor.transpose(
+                    bank[:, q * P : (q + 1) * P], row_words[:, q * P : (q + 1) * P], identity[:]
+                )
+            nc.scalar.copy(
+                out=grouped_words.rearrange("p (g r u) -> p g r u", g=PASSES, u=2),
+                in_=bank[:].rearrange("p (g u r) -> p g r u", g=PASSES, u=2),
+            )
+
+        position = const.tile([P, POS_PER_PART], I32)
+        nc.gpsimd.iota(
+            position[:], pattern=[[1, POS_PER_PART]], base=0, channel_multiplier=POS_PER_PART
+        )
+        identity = const.tile([P, P], F32)
+        make_identity(nc, identity[:])
+
+        rows_of = {0: load_round(0)}
+        w_rows = const.tile([P, D_IN], BF16)
+        nc.sync.dma_start(out=w_rows[:], in_=wqk_w)
+        for r in range(1, LOADS_AHEAD):
+            rows_of[r] = load_round(r)
+
+        turns = const.tile([P, 2, POS_PER_PART, PAIRS], F32)
+        for i in range(PAIRS):
+            nc.vector.tensor_scalar(
+                out=turns[:, 0, :, i],
+                in0=position[:],
+                scalar1=turns_per_position(i),
+                scalar2=None,
+                op0=ALU.mult,
+            )
+        nc.vector.tensor_scalar(
+            out=turns[:, 1], in0=turns[:, 0], scalar1=0.25, scalar2=None, op0=ALU.add
+        )
+        whole_turns = const.tile([P, 2, POS_PER_PART, PAIRS], F32)
+        nc.vector.tensor_scalar(
+            out=whole_turns[:],
+            in0=turns[:],
+            scalar1=ROUND_MAGIC,
+            scalar2=ROUND_MAGIC,
+            op0=ALU.add,
+            op1=ALU.subtract,
+        )
+        part_turns = const.tile([P, 2, POS_PER_PART, PAIRS], F32)
+        nc.vector.tensor_tensor(
+            out=part_turns[:], in0=turns[:], in1=whole_turns[:], op=ALU.subtract
+        )
+
+        w_grouped = const.tile([P, PASSES * D_OUT * 4], BF16, align_bytes=64)
+        w_codes = const.tile([P, PASSES * D_OUT], U32, align_bytes=64)
+        w_scales = const.tile([P, PASSES * D_OUT], U8, align_bytes=64)
+        k_onto_partitions(w_rows[:].bitcast(F32), w_grouped[:].bitcast(F32))
+        nc.vector.quantize_mx(out=w_codes[:].bitcast(FP8X4), scales=w_scales[:], in_=w_grouped[:])
+
+        grouped_of, codes_of, scales_of, sums_of, products_of = {}, {}, {}, {}, {}
+
+        def regroup(r):
+            grouped = mx_pool.tile([P, ROUND_TILES * D_IN], BF16, align_bytes=64)
+            row_words = rows_of[r][:].bitcast(F32)
+            grouped_words = grouped[:].bitcast(F32)
+            for j in range(ROUND_TILES):
+                k_onto_partitions(
+                    row_words[:, j * WORDS : (j + 1) * WORDS],
+                    grouped_words[:, j * WORDS : (j + 1) * WORDS],
+                )
+            grouped_of[r] = grouped
+
+        def quantise(r):
+            codes = mx_pool.tile([P, ROUND_TILES * PASSES * P], U32, align_bytes=64)
+            scales = mx_pool.tile([P, ROUND_TILES * PASSES * P], U8, align_bytes=64)
+            nc.vector.quantize_mx(
+                out=codes[:].bitcast(FP8X4), scales=scales[:], in_=grouped_of[r][:]
+            )
+            codes_of[r], scales_of[r] = codes, scales
+
+        def multiply(r):
+            sums = sum_banks.tile([P, ROUND_OUT], F32)
+            for j in range(ROUND_TILES):
+                for g in range(PASSES):
+                    tokens = slice((j * PASSES + g) * P, (j * PASSES + g + 1) * P)
+                    features = slice(g * D_OUT, (g + 1) * D_OUT)
+                    nc.tensor.matmul_mx(
+                        out=sums[:, j * D_OUT : (j + 1) * D_OUT],
+                        lhsT=codes_of[r][:, tokens].bitcast(FP8X4),
+                        lhsT_scale=scales_of[r][:, tokens],
+                        rhs=w_codes[:, features].bitcast(FP8X4),
+                        rhs_scale=w_scales[:, features],
+                        start=(g == 0),
+                        stop=(g == PASSES - 1),
+                    )
+            sums_of[r] = sums
+
+        def table_of_round(table, r):
+            first = (r % ROUNDS_PER_BATCH) * ROUND_TILES * PAIRS
+            return table[:, first : first + ROUND_TILES * PAIRS].rearrange(
+                "p (j i) -> p j i", j=ROUND_TILES
+            )
+
+        def rotation_products(r):
+            t = sums_of[r][:].rearrange(
+                "p (j c i e) -> p c j i e", j=ROUND_TILES, c=2, e=2
+            )
+            straight = rope_pool.tile([P, 2, ROUND_TILES, PAIRS, 2], F32)
+            crossed = rope_pool.tile([P, 2, 2, ROUND_TILES, PAIRS], F32)
+            per_pair = [P, 2, ROUND_TILES, PAIRS]
+            nc.vector.tensor_tensor(
+                out=crossed[:, 0],
+                in0=t[:, :, :, :, 1],
+                in1=table_of_round(minus_sin, r).unsqueeze(1).to_broadcast(per_pair),
+                op=ALU.mult,
+            )
+            nc.vector.tensor_tensor(
+                out=crossed[:, 1],
+                in0=t[:, :, :, :, 0],
+                in1=table_of_round(sin, r).unsqueeze(1).to_broadcast(per_pair),
+                op=ALU.mult,
+            )
+            nc.vector.tensor_tensor(
+                out=straight[:],
+                in0=t,
+                in1=table_of_round(cos, r).unsqueeze(1).unsqueeze(4).to_broadcast(per_pair + [2]),
+                op=ALU.mult,
+            )
+            products_of[r] = (straight, crossed)
+
+        def rotation_sum_and_store(r):
+            straight, crossed = products_of[r]
+            rotated = out_pool.tile([P, 2, ROUND_TILES * HEAD], F32)
+            nc.vector.tensor_tensor(
+                out=rotated[:].rearrange("p c (n e) -> p (c n) e", e=2),
+                in0=straight[:].rearrange("p c j i e -> p (c j i) e"),
+                in1=crossed[:].rearrange("p e c j i -> p (c j i) e"),
+                op=ALU.add,
+            )
+            batch, part = divmod(r, ROUNDS_PER_BATCH)
+            run = slice(part * ROUND_TILES * HEAD, (part + 1) * ROUND_TILES * HEAD)
+            for c in range(2):
+                nc.sync.dma_start(out=out_runs[c][batch, :, run], in_=rotated[:, c])
+
+        regroup(0)
+        sin = const.tile([P, POS_PER_PART * PAIRS], F32)
+        minus_sin = const.tile([P, POS_PER_PART * PAIRS], F32)
+        cos = const.tile([P, POS_PER_PART * PAIRS], F32)
+        for table, plane, turn in ((sin, 0, 1.0), (minus_sin, 0, -1.0), (cos, 1, 1.0)):
+            nc.scalar.activation(
+                out=table[:],
+                in_=part_turns[:, plane].rearrange("p t i -> p (t i)"),
+                func=ACT.Sin,
+                scale=turn * 2.0 * math.pi,
+            )
+        for s in range(1, ROUNDS + 2):
+            if s + LOADS_AHEAD - 1 < ROUNDS:
+                rows_of[s + LOADS_AHEAD - 1] = load_round(s + LOADS_AHEAD - 1)
+            if s < ROUNDS:
+                regroup(s)
+            if s >= 2:
+                rotation_products(s - 2)
+            if s <= ROUNDS:
+                quantise(s - 1)
+                multiply(s - 1)
+            if s >= 2:
+                rotation_sum_and_store(s - 2)

@@ -23,12 +23,15 @@ ROPE_BASE = 10000.0
 K_PASS = 4 * P
 PASSES = D_IN // K_PASS
 WORDS = D_IN // 2
+BANK = 512
 
 POS_PER_PART = SEQ // P
 ROUND_TILES = 4
 ROUNDS_PER_BATCH = POS_PER_PART // ROUND_TILES
 ROUNDS = BATCH * ROUNDS_PER_BATCH
-ROUND_OUT = ROUND_TILES * D_OUT
+TILE_SUMS = 2 * D_OUT
+BANK_TILES = BANK // TILE_SUMS
+ROUND_BANKS = ROUND_TILES // BANK_TILES
 LOADS_AHEAD = 6
 
 ROUND_MAGIC = 1.5 * 2.0**23
@@ -48,8 +51,8 @@ def tile_attention_pa_t_kernel(tc, x, wqk_w, out_0, out_1):
         mx_pool = ctx.enter_context(tc.tile_pool(name="mx_operands", bufs=3))
         rope_pool = ctx.enter_context(tc.tile_pool(name="rope", bufs=2))
         out_pool = ctx.enter_context(tc.tile_pool(name="rotated", bufs=4))
-        flip_banks = ctx.enter_context(tc.psum_pool(name="flip_banks", bufs=6))
-        sum_banks = ctx.enter_context(tc.psum_pool(name="sum_banks", bufs=2))
+        flip_banks = ctx.enter_context(tc.psum_pool(name="flip_banks", bufs=5))
+        sum_banks = ctx.enter_context(tc.psum_pool(name="sum_banks", bufs=3))
         ctx.enter_context(tc.manual_schedule())
 
         x_runs = x.rearrange("b (p t) d -> b p (t d)", t=POS_PER_PART)
@@ -73,36 +76,52 @@ def tile_attention_pa_t_kernel(tc, x, wqk_w, out_0, out_1):
                     bank[:, q * P : (q + 1) * P], row_words[:, q * P : (q + 1) * P], identity[:]
                 )
             nc.scalar.copy(
-                out=grouped_words.rearrange("p (g r u) -> p g r u", g=PASSES, u=2),
-                in_=bank[:].rearrange("p (g u r) -> p g r u", g=PASSES, u=2),
+                out=grouped_words, in_=bank[:].rearrange("p (g u r) -> p g r u", g=PASSES, u=2)
             )
 
         position = const.tile([P, POS_PER_PART], I32)
         nc.gpsimd.iota(
             position[:], pattern=[[1, POS_PER_PART]], base=0, channel_multiplier=POS_PER_PART
         )
+        partition = const.tile([P, 1], I32)
+        nc.gpsimd.iota(partition[:], pattern=[[0, 1]], base=0, channel_multiplier=1)
         identity = const.tile([P, P], F32)
         make_identity(nc, identity[:])
 
-        rows_of = {0: load_round(0)}
         w_rows = const.tile([P, D_IN], BF16)
         nc.sync.dma_start(out=w_rows[:], in_=wqk_w)
-        for r in range(1, LOADS_AHEAD):
+        partner_rows = const.tile([P, D_IN], BF16)
+        w_halves = wqk_w.rearrange("(n e) k -> e n k", e=2)
+        for e in range(2):
+            nc.sync.dma_start(out=partner_rows[e:P:2, :], in_=w_halves[1 - e])
+        rows_of = {}
+        for r in range(LOADS_AHEAD):
             rows_of[r] = load_round(r)
 
-        turns = const.tile([P, 2, POS_PER_PART, PAIRS], F32)
+        turns = const.tile([P, POS_PER_PART, 2, PAIRS], F32)
         for i in range(PAIRS):
             nc.vector.tensor_scalar(
-                out=turns[:, 0, :, i],
+                out=turns[:, :, 1, i],
                 in0=position[:],
                 scalar1=turns_per_position(i),
                 scalar2=None,
                 op0=ALU.mult,
             )
+        odd_partition = const.tile([P, 1], I32)
         nc.vector.tensor_scalar(
-            out=turns[:, 1], in0=turns[:, 0], scalar1=0.25, scalar2=None, op0=ALU.add
+            out=odd_partition[:], in0=partition[:], scalar1=1, scalar2=None, op0=ALU.bitwise_and
         )
-        whole_turns = const.tile([P, 2, POS_PER_PART, PAIRS], F32)
+        sign = const.tile([P, 1], F32)
+        nc.vector.tensor_scalar(
+            out=sign[:], in0=odd_partition[:], scalar1=2.0, scalar2=-1.0, op0=ALU.mult, op1=ALU.add
+        )
+        nc.vector.tensor_scalar(
+            out=partner_rows[:], in0=partner_rows[:], scalar1=sign[:, 0:1], scalar2=None, op0=ALU.mult
+        )
+        nc.vector.tensor_scalar(
+            out=turns[:, :, 0, :], in0=turns[:, :, 1, :], scalar1=0.25, scalar2=None, op0=ALU.add
+        )
+        whole_turns = const.tile([P, POS_PER_PART, 2, PAIRS], F32)
         nc.vector.tensor_scalar(
             out=whole_turns[:],
             in0=turns[:],
@@ -111,15 +130,19 @@ def tile_attention_pa_t_kernel(tc, x, wqk_w, out_0, out_1):
             op0=ALU.add,
             op1=ALU.subtract,
         )
-        part_turns = const.tile([P, 2, POS_PER_PART, PAIRS], F32)
+        part_turns = const.tile([P, POS_PER_PART, 2, PAIRS], F32)
         nc.vector.tensor_tensor(
             out=part_turns[:], in0=turns[:], in1=whole_turns[:], op=ALU.subtract
         )
 
-        w_grouped = const.tile([P, PASSES * D_OUT * 4], BF16, align_bytes=64)
-        w_codes = const.tile([P, PASSES * D_OUT], U32, align_bytes=64)
-        w_scales = const.tile([P, PASSES * D_OUT], U8, align_bytes=64)
-        k_onto_partitions(w_rows[:].bitcast(F32), w_grouped[:].bitcast(F32))
+        w_grouped = const.tile([P, PASSES * TILE_SUMS * 4], BF16, align_bytes=64)
+        w_codes = const.tile([P, PASSES * TILE_SUMS], U32, align_bytes=64)
+        w_scales = const.tile([P, PASSES * TILE_SUMS], U8, align_bytes=64)
+        w_grouped_words = w_grouped[:].bitcast(F32).rearrange(
+            "p (g h r u) -> p h g r u", g=PASSES, h=2, u=2
+        )
+        k_onto_partitions(w_rows[:].bitcast(F32), w_grouped_words[:, 0])
+        k_onto_partitions(partner_rows[:].bitcast(F32), w_grouped_words[:, 1])
         nc.vector.quantize_mx(out=w_codes[:].bitcast(FP8X4), scales=w_scales[:], in_=w_grouped[:])
 
         grouped_of, codes_of, scales_of, sums_of, products_of = {}, {}, {}, {}, {}
@@ -127,13 +150,27 @@ def tile_attention_pa_t_kernel(tc, x, wqk_w, out_0, out_1):
         def regroup(r):
             grouped = mx_pool.tile([P, ROUND_TILES * D_IN], BF16, align_bytes=64)
             row_words = rows_of[r][:].bitcast(F32)
-            grouped_words = grouped[:].bitcast(F32)
+            grouped_words = grouped[:].bitcast(F32).rearrange(
+                "p (j g r u) -> p j g r u", j=ROUND_TILES, g=PASSES, u=2
+            )
             for j in range(ROUND_TILES):
-                k_onto_partitions(
-                    row_words[:, j * WORDS : (j + 1) * WORDS],
-                    grouped_words[:, j * WORDS : (j + 1) * WORDS],
-                )
+                k_onto_partitions(row_words[:, j * WORDS : (j + 1) * WORDS], grouped_words[:, j])
             grouped_of[r] = grouped
+
+        cos_sin = const.tile([P, POS_PER_PART * 2 * PAIRS, 2], F32)
+        ROUND_FACTORS = ROUND_TILES * 2 * PAIRS
+
+        def factors_for_round(n):
+            these = slice(n * ROUND_FACTORS, (n + 1) * ROUND_FACTORS)
+            nc.scalar.activation(
+                out=cos_sin[:, these, :],
+                in_=part_turns[:]
+                .rearrange("p t h i -> p (t h i)")[:, these]
+                .unsqueeze(2)
+                .to_broadcast([P, ROUND_FACTORS, 2]),
+                func=ACT.Sin,
+                scale=2.0 * math.pi,
+            )
 
         def quantise(r):
             codes = mx_pool.tile([P, ROUND_TILES * PASSES * P], U32, align_bytes=64)
@@ -144,88 +181,62 @@ def tile_attention_pa_t_kernel(tc, x, wqk_w, out_0, out_1):
             codes_of[r], scales_of[r] = codes, scales
 
         def multiply(r):
-            sums = sum_banks.tile([P, ROUND_OUT], F32)
-            for j in range(ROUND_TILES):
-                for g in range(PASSES):
-                    tokens = slice((j * PASSES + g) * P, (j * PASSES + g + 1) * P)
-                    features = slice(g * D_OUT, (g + 1) * D_OUT)
-                    nc.tensor.matmul_mx(
-                        out=sums[:, j * D_OUT : (j + 1) * D_OUT],
-                        lhsT=codes_of[r][:, tokens].bitcast(FP8X4),
-                        lhsT_scale=scales_of[r][:, tokens],
-                        rhs=w_codes[:, features].bitcast(FP8X4),
-                        rhs_scale=w_scales[:, features],
-                        start=(g == 0),
-                        stop=(g == PASSES - 1),
-                    )
-            sums_of[r] = sums
-
-        def table_of_round(table, r):
-            first = (r % ROUNDS_PER_BATCH) * ROUND_TILES * PAIRS
-            return table[:, first : first + ROUND_TILES * PAIRS].rearrange(
-                "p (j i) -> p j i", j=ROUND_TILES
-            )
+            sums_of[r] = []
+            for first_tile in range(0, ROUND_TILES, BANK_TILES):
+                sums = sum_banks.tile([P, BANK], F32)
+                for j in range(BANK_TILES):
+                    for g in range(PASSES):
+                        at = ((first_tile + j) * PASSES + g) * P
+                        nc.tensor.matmul_mx(
+                            out=sums[:, j * TILE_SUMS : (j + 1) * TILE_SUMS],
+                            lhsT=codes_of[r][:, at : at + P].bitcast(FP8X4),
+                            lhsT_scale=scales_of[r][:, at : at + P],
+                            rhs=w_codes[:, g * TILE_SUMS : (g + 1) * TILE_SUMS].bitcast(FP8X4),
+                            rhs_scale=w_scales[:, g * TILE_SUMS : (g + 1) * TILE_SUMS],
+                            start=(g == 0),
+                            stop=(g == PASSES - 1),
+                        )
+                sums_of[r].append(sums)
 
         def rotation_products(r):
-            t = sums_of[r][:].rearrange(
-                "p (j c i e) -> p c j i e", j=ROUND_TILES, c=2, e=2
-            )
-            straight = rope_pool.tile([P, 2, ROUND_TILES, PAIRS, 2], F32)
-            crossed = rope_pool.tile([P, 2, 2, ROUND_TILES, PAIRS], F32)
-            per_pair = [P, 2, ROUND_TILES, PAIRS]
-            nc.vector.tensor_tensor(
-                out=crossed[:, 0],
-                in0=t[:, :, :, :, 1],
-                in1=table_of_round(minus_sin, r).unsqueeze(1).to_broadcast(per_pair),
-                op=ALU.mult,
-            )
-            nc.vector.tensor_tensor(
-                out=crossed[:, 1],
-                in0=t[:, :, :, :, 0],
-                in1=table_of_round(sin, r).unsqueeze(1).to_broadcast(per_pair),
-                op=ALU.mult,
-            )
-            nc.vector.tensor_tensor(
-                out=straight[:],
-                in0=t,
-                in1=table_of_round(cos, r).unsqueeze(1).unsqueeze(4).to_broadcast(per_pair + [2]),
-                op=ALU.mult,
-            )
-            products_of[r] = (straight, crossed)
+            products = rope_pool.tile([P, ROUND_TILES * 2, 2, HEAD], F32)
+            bank_rows = BANK_TILES * 2
+            first = (r % ROUNDS_PER_BATCH) * ROUND_TILES * 2
+            factors = cos_sin[:].rearrange("p (th i) e -> p th (i e)", i=PAIRS)
+            for b, sums in enumerate(sums_of[r]):
+                nc.vector.tensor_tensor(
+                    out=products[:, b * bank_rows : (b + 1) * bank_rows],
+                    in0=sums[:].rearrange("p (th c f) -> p th c f", c=2, f=HEAD),
+                    in1=factors[:, first + b * bank_rows : first + (b + 1) * bank_rows]
+                    .unsqueeze(2)
+                    .to_broadcast([P, bank_rows, 2, HEAD]),
+                    op=ALU.mult,
+                )
+            products_of[r] = products
 
         def rotation_sum_and_store(r):
-            straight, crossed = products_of[r]
-            rotated = out_pool.tile([P, 2, ROUND_TILES * HEAD], F32)
+            by_term = products_of[r][:].rearrange("p (j h) c f -> p h c j f", h=2)
+            rotated = out_pool.tile([P, 2, ROUND_TILES, HEAD], F32)
             nc.vector.tensor_tensor(
-                out=rotated[:].rearrange("p c (n e) -> p (c n) e", e=2),
-                in0=straight[:].rearrange("p c j i e -> p (c j i) e"),
-                in1=crossed[:].rearrange("p e c j i -> p (c j i) e"),
-                op=ALU.add,
+                out=rotated[:], in0=by_term[:, 0], in1=by_term[:, 1], op=ALU.add
             )
             batch, part = divmod(r, ROUNDS_PER_BATCH)
             run = slice(part * ROUND_TILES * HEAD, (part + 1) * ROUND_TILES * HEAD)
             for c in range(2):
-                nc.sync.dma_start(out=out_runs[c][batch, :, run], in_=rotated[:, c])
+                nc.sync.dma_start(
+                    out=out_runs[c][batch, :, run], in_=rotated[:, c].rearrange("p j f -> p (j f)")
+                )
 
-        regroup(0)
-        sin = const.tile([P, POS_PER_PART * PAIRS], F32)
-        minus_sin = const.tile([P, POS_PER_PART * PAIRS], F32)
-        cos = const.tile([P, POS_PER_PART * PAIRS], F32)
-        for table, plane, turn in ((sin, 0, 1.0), (minus_sin, 0, -1.0), (cos, 1, 1.0)):
-            nc.scalar.activation(
-                out=table[:],
-                in_=part_turns[:, plane].rearrange("p t i -> p (t i)"),
-                func=ACT.Sin,
-                scale=turn * 2.0 * math.pi,
-            )
-        for s in range(1, ROUNDS + 2):
-            if s + LOADS_AHEAD - 1 < ROUNDS:
+        for s in range(ROUNDS + 2):
+            if LOADS_AHEAD <= s + LOADS_AHEAD - 1 < ROUNDS:
                 rows_of[s + LOADS_AHEAD - 1] = load_round(s + LOADS_AHEAD - 1)
             if s < ROUNDS:
                 regroup(s)
+            if s < ROUNDS_PER_BATCH:
+                factors_for_round(s)
             if s >= 2:
                 rotation_products(s - 2)
-            if s <= ROUNDS:
+            if 1 <= s <= ROUNDS:
                 quantise(s - 1)
                 multiply(s - 1)
             if s >= 2:

@@ -227,17 +227,17 @@ def tile_attention_pa_t_kernel(tc, x, wqk_w, out_0, out_1):
                     out=out_runs[c][batch, :, run], in_=rotated[:, c].rearrange("p j f -> p (j f)")
                 )
 
-        for s in range(ROUNDS + 2):
+        for s in range(ROUNDS + 3):
             if LOADS_AHEAD <= s + LOADS_AHEAD - 1 < ROUNDS:
                 rows_of[s + LOADS_AHEAD - 1] = load_round(s + LOADS_AHEAD - 1)
             if s < ROUNDS:
                 regroup(s)
             if s < ROUNDS_PER_BATCH:
                 factors_for_round(s)
-            if s >= 2:
-                rotation_products(s - 2)
             if 1 <= s <= ROUNDS:
                 quantise(s - 1)
                 multiply(s - 1)
-            if s >= 2:
-                rotation_sum_and_store(s - 2)
+            if 2 <= s < ROUNDS + 2:
+                rotation_products(s - 2)
+            if s >= 3:
+                rotation_sum_and_store(s - 3)

@@ -33,6 +33,7 @@ TILE_SUMS = 2 * D_OUT
 BANK_TILES = BANK // TILE_SUMS
 ROUND_BANKS = ROUND_TILES // BANK_TILES
 LOADS_AHEAD = 6
+FIRST_LOAD_PIECES = ROUND_TILES
 
 ROUND_MAGIC = 1.5 * 2.0**23
 
@@ -60,13 +61,16 @@ def tile_attention_pa_t_kernel(tc, x, wqk_w, out_0, out_1):
             out.rearrange("b h (p t) f -> (b h) p (t f)", t=POS_PER_PART) for out in (out_0, out_1)
         ]
 
-        def load_round(r):
+        def load_round(r, pieces):
             batch, part = divmod(r, ROUNDS_PER_BATCH)
             rows = row_pool.tile([P, ROUND_TILES * D_IN], BF16)
-            nc.sync.dma_start(
-                out=rows[:],
-                in_=x_runs[batch, :, part * ROUND_TILES * D_IN : (part + 1) * ROUND_TILES * D_IN],
-            )
+            width = ROUND_TILES * D_IN // pieces
+            for piece in range(pieces):
+                start = (part * pieces + piece) * width
+                nc.sync.dma_start(
+                    out=rows[:, piece * width : (piece + 1) * width],
+                    in_=x_runs[batch, :, start : start + width],
+                )
             return rows
 
         def k_onto_partitions(row_words, grouped_words):
@@ -88,15 +92,15 @@ def tile_attention_pa_t_kernel(tc, x, wqk_w, out_0, out_1):
         identity = const.tile([P, P], F32)
         make_identity(nc, identity[:])
 
+        rows_of = {0: load_round(0, FIRST_LOAD_PIECES)}
         w_rows = const.tile([P, D_IN], BF16)
         nc.sync.dma_start(out=w_rows[:], in_=wqk_w)
         partner_rows = const.tile([P, D_IN], BF16)
         w_halves = wqk_w.rearrange("(n e) k -> e n k", e=2)
         for e in range(2):
             nc.sync.dma_start(out=partner_rows[e:P:2, :], in_=w_halves[1 - e])
-        rows_of = {}
-        for r in range(LOADS_AHEAD):
-            rows_of[r] = load_round(r)
+        for r in range(1, LOADS_AHEAD):
+            rows_of[r] = load_round(r, 1)
 
         turns = const.tile([P, POS_PER_PART, 2, PAIRS], F32)
         for i in range(PAIRS):
@@ -107,17 +111,6 @@ def tile_attention_pa_t_kernel(tc, x, wqk_w, out_0, out_1):
                 scalar2=None,
                 op0=ALU.mult,
             )
-        odd_partition = const.tile([P, 1], I32)
-        nc.vector.tensor_scalar(
-            out=odd_partition[:], in0=partition[:], scalar1=1, scalar2=None, op0=ALU.bitwise_and
-        )
-        sign = const.tile([P, 1], F32)
-        nc.vector.tensor_scalar(
-            out=sign[:], in0=odd_partition[:], scalar1=2.0, scalar2=-1.0, op0=ALU.mult, op1=ALU.add
-        )
-        nc.vector.tensor_scalar(
-            out=partner_rows[:], in0=partner_rows[:], scalar1=sign[:, 0:1], scalar2=None, op0=ALU.mult
-        )
         nc.vector.tensor_scalar(
             out=turns[:, :, 0, :], in0=turns[:, :, 1, :], scalar1=0.25, scalar2=None, op0=ALU.add
         )
@@ -138,12 +131,31 @@ def tile_attention_pa_t_kernel(tc, x, wqk_w, out_0, out_1):
         w_grouped = const.tile([P, PASSES * TILE_SUMS * 4], BF16, align_bytes=64)
         w_codes = const.tile([P, PASSES * TILE_SUMS], U32, align_bytes=64)
         w_scales = const.tile([P, PASSES * TILE_SUMS], U8, align_bytes=64)
-        w_grouped_words = w_grouped[:].bitcast(F32).rearrange(
-            "p (g h r u) -> p h g r u", g=PASSES, h=2, u=2
-        )
-        k_onto_partitions(w_rows[:].bitcast(F32), w_grouped_words[:, 0])
-        k_onto_partitions(partner_rows[:].bitcast(F32), w_grouped_words[:, 1])
-        nc.vector.quantize_mx(out=w_codes[:].bitcast(FP8X4), scales=w_scales[:], in_=w_grouped[:])
+
+        def prepare_weights():
+            odd_partition = const.tile([P, 1], I32)
+            nc.vector.tensor_scalar(
+                out=odd_partition[:], in0=partition[:], scalar1=1, scalar2=None, op0=ALU.bitwise_and
+            )
+            sign = const.tile([P, 1], F32)
+            nc.vector.tensor_scalar(
+                out=sign[:], in0=odd_partition[:], scalar1=2.0, scalar2=-1.0, op0=ALU.mult, op1=ALU.add
+            )
+            nc.vector.tensor_scalar(
+                out=partner_rows[:],
+                in0=partner_rows[:],
+                scalar1=sign[:, 0:1],
+                scalar2=None,
+                op0=ALU.mult,
+            )
+            w_grouped_words = w_grouped[:].bitcast(F32).rearrange(
+                "p (g h r u) -> p h g r u", g=PASSES, h=2, u=2
+            )
+            k_onto_partitions(w_rows[:].bitcast(F32), w_grouped_words[:, 0])
+            k_onto_partitions(partner_rows[:].bitcast(F32), w_grouped_words[:, 1])
+            nc.vector.quantize_mx(
+                out=w_codes[:].bitcast(FP8X4), scales=w_scales[:], in_=w_grouped[:]
+            )
 
         grouped_of, codes_of, scales_of, sums_of, products_of = {}, {}, {}, {}, {}
 
@@ -217,27 +229,31 @@ def tile_attention_pa_t_kernel(tc, x, wqk_w, out_0, out_1):
         def rotation_sum_and_store(r):
             by_term = products_of[r][:].rearrange("p (j h) c f -> p h c j f", h=2)
             rotated = out_pool.tile([P, 2, ROUND_TILES, HEAD], F32)
-            nc.vector.tensor_tensor(
-                out=rotated[:], in0=by_term[:, 0], in1=by_term[:, 1], op=ALU.add
-            )
             batch, part = divmod(r, ROUNDS_PER_BATCH)
             run = slice(part * ROUND_TILES * HEAD, (part + 1) * ROUND_TILES * HEAD)
             for c in range(2):
+                nc.gpsimd.tensor_tensor(
+                    out=rotated[:, c], in0=by_term[:, 0, c], in1=by_term[:, 1, c], op=ALU.add
+                )
                 nc.sync.dma_start(
                     out=out_runs[c][batch, :, run], in_=rotated[:, c].rearrange("p j f -> p (j f)")
                 )
 
-        for s in range(ROUNDS + 3):
-            if LOADS_AHEAD <= s + LOADS_AHEAD - 1 < ROUNDS:
-                rows_of[s + LOADS_AHEAD - 1] = load_round(s + LOADS_AHEAD - 1)
+        regroup(0)
+        prepare_weights()
+        factors_for_round(0)
+        for s in range(1, ROUNDS + 3):
+            if s + LOADS_AHEAD - 1 < ROUNDS:
+                rows_of[s + LOADS_AHEAD - 1] = load_round(s + LOADS_AHEAD - 1, 1)
             if s < ROUNDS:
                 regroup(s)
             if s < ROUNDS_PER_BATCH:
                 factors_for_round(s)
-            if 1 <= s <= ROUNDS:
-                quantise(s - 1)
-                multiply(s - 1)
             if 2 <= s < ROUNDS + 2:
-                rotation_products(s - 2)
+                multiply(s - 2)
+            if s >= 3:
+                rotation_products(s - 3)
+            if s <= ROUNDS:
+                quantise(s - 1)
             if s >= 3:
                 rotation_sum_and_store(s - 3)

@@ -157,7 +157,7 @@ def tile_attention_pa_t_kernel(tc, x, wqk_w, out_0, out_1):
                 out=w_codes[:].bitcast(FP8X4), scales=w_scales[:], in_=w_grouped[:]
             )
 
-        grouped_of, codes_of, scales_of, sums_of, products_of = {}, {}, {}, {}, {}
+        grouped_of, codes_of, scales_of, sums_of, products_of, rotated_of = {}, {}, {}, {}, {}, {}
 
         def regroup(r):
             grouped = mx_pool.tile([P, ROUND_TILES * D_IN], BF16, align_bytes=64)
@@ -184,13 +184,17 @@ def tile_attention_pa_t_kernel(tc, x, wqk_w, out_0, out_1):
                 scale=2.0 * math.pi,
             )
 
-        def quantise(r):
-            codes = mx_pool.tile([P, ROUND_TILES * PASSES * P], U32, align_bytes=64)
-            scales = mx_pool.tile([P, ROUND_TILES * PASSES * P], U8, align_bytes=64)
+        def quantise(r, half):
+            if half == 0:
+                codes = mx_pool.tile([P, ROUND_TILES * PASSES * P], U32, align_bytes=64)
+                scales = mx_pool.tile([P, ROUND_TILES * PASSES * P], U8, align_bytes=64)
+                codes_of[r], scales_of[r] = codes, scales
+            words = BANK_TILES * PASSES * P
             nc.vector.quantize_mx(
-                out=codes[:].bitcast(FP8X4), scales=scales[:], in_=grouped_of[r][:]
+                out=codes_of[r][:, half * words : (half + 1) * words].bitcast(FP8X4),
+                scales=scales_of[r][:, half * words : (half + 1) * words],
+                in_=grouped_of[r][:, half * 4 * words : (half + 1) * 4 * words],
             )
-            codes_of[r], scales_of[r] = codes, scales
 
         def multiply(r):
             sums_of[r] = []
@@ -210,50 +214,56 @@ def tile_attention_pa_t_kernel(tc, x, wqk_w, out_0, out_1):
                         )
                 sums_of[r].append(sums)
 
-        def rotation_products(r):
-            products = rope_pool.tile([P, ROUND_TILES * 2, 2, HEAD], F32)
+        def rotate_half(r, half):
+            if half == 0:
+                products = rope_pool.tile([P, ROUND_TILES * 2, 2, HEAD], F32)
+                rotated = out_pool.tile([P, 2, ROUND_TILES, HEAD], F32)
+                products_of[r], rotated_of[r] = products, rotated
             bank_rows = BANK_TILES * 2
-            first = (r % ROUNDS_PER_BATCH) * ROUND_TILES * 2
+            first = (r % ROUNDS_PER_BATCH) * ROUND_TILES * 2 + half * bank_rows
             factors = cos_sin[:].rearrange("p (th i) e -> p th (i e)", i=PAIRS)
-            for b, sums in enumerate(sums_of[r]):
-                nc.vector.tensor_tensor(
-                    out=products[:, b * bank_rows : (b + 1) * bank_rows],
-                    in0=sums[:].rearrange("p (th c f) -> p th c f", c=2, f=HEAD),
-                    in1=factors[:, first + b * bank_rows : first + (b + 1) * bank_rows]
-                    .unsqueeze(2)
-                    .to_broadcast([P, bank_rows, 2, HEAD]),
-                    op=ALU.mult,
-                )
-            products_of[r] = products
-
-        def rotation_sum_and_store(r):
+            nc.vector.tensor_tensor(
+                out=products_of[r][:, half * bank_rows : (half + 1) * bank_rows],
+                in0=sums_of[r][half][:].rearrange("p (th c f) -> p th c f", c=2, f=HEAD),
+                in1=factors[:, first : first + bank_rows]
+                .unsqueeze(2)
+                .to_broadcast([P, bank_rows, 2, HEAD]),
+                op=ALU.mult,
+            )
+            tiles = slice(half * BANK_TILES, (half + 1) * BANK_TILES)
             by_term = products_of[r][:].rearrange("p (j h) c f -> p h c j f", h=2)
-            rotated = out_pool.tile([P, 2, ROUND_TILES, HEAD], F32)
+            nc.gpsimd.tensor_tensor(
+                out=rotated_of[r][:, :, tiles, :],
+                in0=by_term[:, 0, :, tiles, :],
+                in1=by_term[:, 1, :, tiles, :],
+                op=ALU.add,
+            )
+
+        def store(r):
             batch, part = divmod(r, ROUNDS_PER_BATCH)
             run = slice(part * ROUND_TILES * HEAD, (part + 1) * ROUND_TILES * HEAD)
             for c in range(2):
-                nc.gpsimd.tensor_tensor(
-                    out=rotated[:, c], in0=by_term[:, 0, c], in1=by_term[:, 1, c], op=ALU.add
-                )
                 nc.sync.dma_start(
-                    out=out_runs[c][batch, :, run], in_=rotated[:, c].rearrange("p j f -> p (j f)")
+                    out=out_runs[c][batch, :, run],
+                    in_=rotated_of[r][:, c].rearrange("p j f -> p (j f)"),
                 )
 
         regroup(0)
         prepare_weights()
         factors_for_round(0)
-        for s in range(1, ROUNDS + 3):
+        for s in range(1, ROUNDS + 2):
             if s + LOADS_AHEAD - 1 < ROUNDS:
                 rows_of[s + LOADS_AHEAD - 1] = load_round(s + LOADS_AHEAD - 1, 1)
             if s < ROUNDS:
                 regroup(s)
             if s < ROUNDS_PER_BATCH:
                 factors_for_round(s)
-            if 2 <= s < ROUNDS + 2:
-                multiply(s - 2)
-            if s >= 3:
-                rotation_products(s - 3)
+            for half in range(ROUND_BANKS):
+                if s <= ROUNDS:
+                    quantise(s - 1, half)
+                if s >= 2:
+                    rotate_half(s - 2, half)
             if s <= ROUNDS:
-                quantise(s - 1)
-            if s >= 3:
-                rotation_sum_and_store(s - 3)
+                multiply(s - 1)
+            if s >= 2:
+                store(s - 2)

@@ -92,13 +92,13 @@ def tile_attention_pa_t_kernel(tc, x, wqk_w, out_0, out_1):
         identity = const.tile([P, P], F32)
         make_identity(nc, identity[:])
 
-        rows_of = {0: load_round(0, FIRST_LOAD_PIECES)}
         w_rows = const.tile([P, D_IN], BF16)
         nc.sync.dma_start(out=w_rows[:], in_=wqk_w)
         partner_rows = const.tile([P, D_IN], BF16)
         w_halves = wqk_w.rearrange("(n e) k -> e n k", e=2)
         for e in range(2):
             nc.sync.dma_start(out=partner_rows[e:P:2, :], in_=w_halves[1 - e])
+        rows_of = {0: load_round(0, FIRST_LOAD_PIECES)}
         for r in range(1, LOADS_AHEAD):
             rows_of[r] = load_round(r, 1)
 
@@ -111,6 +111,17 @@ def tile_attention_pa_t_kernel(tc, x, wqk_w, out_0, out_1):
                 scalar2=None,
                 op0=ALU.mult,
             )
+        odd_partition = const.tile([P, 1], I32)
+        nc.vector.tensor_scalar(
+            out=odd_partition[:], in0=partition[:], scalar1=1, scalar2=None, op0=ALU.bitwise_and
+        )
+        sign = const.tile([P, 1], F32)
+        nc.vector.tensor_scalar(
+            out=sign[:], in0=odd_partition[:], scalar1=2.0, scalar2=-1.0, op0=ALU.mult, op1=ALU.add
+        )
+        nc.vector.tensor_scalar(
+            out=partner_rows[:], in0=partner_rows[:], scalar1=sign[:, 0:1], scalar2=None, op0=ALU.mult
+        )
         nc.vector.tensor_scalar(
             out=turns[:, :, 0, :], in0=turns[:, :, 1, :], scalar1=0.25, scalar2=None, op0=ALU.add
         )
@@ -133,21 +144,6 @@ def tile_attention_pa_t_kernel(tc, x, wqk_w, out_0, out_1):
         w_scales = const.tile([P, PASSES * TILE_SUMS], U8, align_bytes=64)
 
         def prepare_weights():
-            odd_partition = const.tile([P, 1], I32)
-            nc.vector.tensor_scalar(
-                out=odd_partition[:], in0=partition[:], scalar1=1, scalar2=None, op0=ALU.bitwise_and
-            )
-            sign = const.tile([P, 1], F32)
-            nc.vector.tensor_scalar(
-                out=sign[:], in0=odd_partition[:], scalar1=2.0, scalar2=-1.0, op0=ALU.mult, op1=ALU.add
-            )
-            nc.vector.tensor_scalar(
-                out=partner_rows[:],
-                in0=partner_rows[:],
-                scalar1=sign[:, 0:1],
-                scalar2=None,
-                op0=ALU.mult,
-            )
             w_grouped_words = w_grouped[:].bitcast(F32).rearrange(
                 "p (g h r u) -> p h g r u", g=PASSES, h=2, u=2
             )
@@ -248,12 +244,17 @@ def tile_attention_pa_t_kernel(tc, x, wqk_w, out_0, out_1):
                     in_=rotated_of[r][:, c].rearrange("p j f -> p (j f)"),
                 )
 
-        regroup(0)
         prepare_weights()
+        regroup(0)
         factors_for_round(0)
-        for s in range(1, ROUNDS + 2):
-            if s + LOADS_AHEAD - 1 < ROUNDS:
-                rows_of[s + LOADS_AHEAD - 1] = load_round(s + LOADS_AHEAD - 1, 1)
+        for half in range(ROUND_BANKS):
+            quantise(0, half)
+        multiply(0)
+        regroup(1)
+        factors_for_round(1)
+        for s in range(2, ROUNDS + 2):
+            if s + LOADS_AHEAD - 2 < ROUNDS:
+                rows_of[s + LOADS_AHEAD - 2] = load_round(s + LOADS_AHEAD - 2, 1)
             if s < ROUNDS:
                 regroup(s)
             if s < ROUNDS_PER_BATCH:
@@ -261,9 +262,7 @@ def tile_attention_pa_t_kernel(tc, x, wqk_w, out_0, out_1):
             for half in range(ROUND_BANKS):
                 if s <= ROUNDS:
                     quantise(s - 1, half)
-                if s >= 2:
-                    rotate_half(s - 2, half)
+                rotate_half(s - 2, half)
             if s <= ROUNDS:
                 multiply(s - 1)
-            if s >= 2:
-                store(s - 2)
+            store(s - 2)

@@ -32,7 +32,7 @@ ROUNDS = BATCH * ROUNDS_PER_BATCH
 TILE_SUMS = 2 * D_OUT
 BANK_TILES = BANK // TILE_SUMS
 ROUND_BANKS = ROUND_TILES // BANK_TILES
-LOADS_AHEAD = 6
+LOADS_AHEAD = 10
 FIRST_LOAD_PIECES = ROUND_TILES
 
 ROUND_MAGIC = 1.5 * 2.0**23
@@ -51,7 +51,7 @@ def tile_attention_pa_t_kernel(tc, x, wqk_w, out_0, out_1):
         row_pool = ctx.enter_context(tc.tile_pool(name="rows", bufs=LOADS_AHEAD + 2))
         mx_pool = ctx.enter_context(tc.tile_pool(name="mx_operands", bufs=3))
         rope_pool = ctx.enter_context(tc.tile_pool(name="rope", bufs=2))
-        out_pool = ctx.enter_context(tc.tile_pool(name="rotated", bufs=4))
+        out_pool = ctx.enter_context(tc.tile_pool(name="rotated", bufs=8))
         flip_banks = ctx.enter_context(tc.psum_pool(name="flip_banks", bufs=5))
         sum_banks = ctx.enter_context(tc.psum_pool(name="sum_banks", bufs=3))
         ctx.enter_context(tc.manual_schedule())
@@ -92,13 +92,13 @@ def tile_attention_pa_t_kernel(tc, x, wqk_w, out_0, out_1):
         identity = const.tile([P, P], F32)
         make_identity(nc, identity[:])
 
+        rows_of = {0: load_round(0, FIRST_LOAD_PIECES)}
         w_rows = const.tile([P, D_IN], BF16)
         nc.sync.dma_start(out=w_rows[:], in_=wqk_w)
         partner_rows = const.tile([P, D_IN], BF16)
         w_halves = wqk_w.rearrange("(n e) k -> e n k", e=2)
         for e in range(2):
             nc.sync.dma_start(out=partner_rows[e:P:2, :], in_=w_halves[1 - e])
-        rows_of = {0: load_round(0, FIRST_LOAD_PIECES)}
         for r in range(1, LOADS_AHEAD):
             rows_of[r] = load_round(r, 1)
 
@@ -111,17 +111,6 @@ def tile_attention_pa_t_kernel(tc, x, wqk_w, out_0, out_1):
                 scalar2=None,
                 op0=ALU.mult,
             )
-        odd_partition = const.tile([P, 1], I32)
-        nc.vector.tensor_scalar(
-            out=odd_partition[:], in0=partition[:], scalar1=1, scalar2=None, op0=ALU.bitwise_and
-        )
-        sign = const.tile([P, 1], F32)
-        nc.vector.tensor_scalar(
-            out=sign[:], in0=odd_partition[:], scalar1=2.0, scalar2=-1.0, op0=ALU.mult, op1=ALU.add
-        )
-        nc.vector.tensor_scalar(
-            out=partner_rows[:], in0=partner_rows[:], scalar1=sign[:, 0:1], scalar2=None, op0=ALU.mult
-        )
         nc.vector.tensor_scalar(
             out=turns[:, :, 0, :], in0=turns[:, :, 1, :], scalar1=0.25, scalar2=None, op0=ALU.add
         )
@@ -144,6 +133,21 @@ def tile_attention_pa_t_kernel(tc, x, wqk_w, out_0, out_1):
         w_scales = const.tile([P, PASSES * TILE_SUMS], U8, align_bytes=64)
 
         def prepare_weights():
+            odd_partition = const.tile([P, 1], I32)
+            nc.vector.tensor_scalar(
+                out=odd_partition[:], in0=partition[:], scalar1=1, scalar2=None, op0=ALU.bitwise_and
+            )
+            sign = const.tile([P, 1], F32)
+            nc.vector.tensor_scalar(
+                out=sign[:], in0=odd_partition[:], scalar1=2.0, scalar2=-1.0, op0=ALU.mult, op1=ALU.add
+            )
+            nc.vector.tensor_scalar(
+                out=partner_rows[:],
+                in0=partner_rows[:],
+                scalar1=sign[:, 0:1],
+                scalar2=None,
+                op0=ALU.mult,
+            )
             w_grouped_words = w_grouped[:].bitcast(F32).rearrange(
                 "p (g h r u) -> p h g r u", g=PASSES, h=2, u=2
             )
@@ -244,17 +248,12 @@ def tile_attention_pa_t_kernel(tc, x, wqk_w, out_0, out_1):
                     in_=rotated_of[r][:, c].rearrange("p j f -> p (j f)"),
                 )
 
-        prepare_weights()
         regroup(0)
+        prepare_weights()
         factors_for_round(0)
-        for half in range(ROUND_BANKS):
-            quantise(0, half)
-        multiply(0)
-        regroup(1)
-        factors_for_round(1)
-        for s in range(2, ROUNDS + 2):
-            if s + LOADS_AHEAD - 2 < ROUNDS:
-                rows_of[s + LOADS_AHEAD - 2] = load_round(s + LOADS_AHEAD - 2, 1)
+        for s in range(1, ROUNDS + 2):
+            if s + LOADS_AHEAD - 1 < ROUNDS:
+                rows_of[s + LOADS_AHEAD - 1] = load_round(s + LOADS_AHEAD - 1, 1)
             if s < ROUNDS:
                 regroup(s)
             if s < ROUNDS_PER_BATCH:
@@ -262,7 +261,9 @@ def tile_attention_pa_t_kernel(tc, x, wqk_w, out_0, out_1):
             for half in range(ROUND_BANKS):
                 if s <= ROUNDS:
                     quantise(s - 1, half)
-                rotate_half(s - 2, half)
+                if s >= 2:
+                    rotate_half(s - 2, half)
             if s <= ROUNDS:
                 multiply(s - 1)
-            store(s - 2)
+            if s >= 2:
+                store(s - 2)

import math
from contextlib import ExitStack

import concourse.mybir as mybir
from concourse.masks import make_identity

F32 = mybir.dt.float32
BF16 = mybir.dt.bfloat16
I32 = mybir.dt.int32
U32 = mybir.dt.uint32
U8 = mybir.dt.uint8
FP8X4 = mybir.dt.float8_e4m3fn_x4
ALU = mybir.AluOpType
ACT = mybir.ActivationFunctionType

P = 128
BATCH, SEQ, D_IN = 4, 2048, 1024
HEAD = 64
PAIRS = HEAD // 2
D_OUT = 2 * HEAD
ROPE_BASE = 10000.0

K_PASS = 4 * P
PASSES = D_IN // K_PASS
WORDS = D_IN // 2
BANK = 512

POS_PER_PART = SEQ // P
ROUND_TILES = 4
ROUNDS_PER_BATCH = POS_PER_PART // ROUND_TILES
ROUNDS = BATCH * ROUNDS_PER_BATCH
TILE_SUMS = 2 * D_OUT
BANK_TILES = BANK // TILE_SUMS
ROUND_BANKS = ROUND_TILES // BANK_TILES
LOADS_AHEAD = 10
FIRST_LOAD_PIECES = ROUND_TILES

ROUND_MAGIC = 1.5 * 2.0**23

FLOPS = 2 * BATCH * SEQ * D_IN * D_OUT


def turns_per_position(i):
    return 1.0 / (ROPE_BASE ** (2.0 * i / HEAD) * 2.0 * math.pi)


def tile_attention_pa_t_kernel(tc, x, wqk_w, out_0, out_1):
    nc = tc.nc
    with ExitStack() as ctx:
        const = ctx.enter_context(tc.tile_pool(name="const", bufs=1))
        row_pool = ctx.enter_context(tc.tile_pool(name="rows", bufs=LOADS_AHEAD + 2))
        mx_pool = ctx.enter_context(tc.tile_pool(name="mx_operands", bufs=3))
        rope_pool = ctx.enter_context(tc.tile_pool(name="rope", bufs=2))
        out_pool = ctx.enter_context(tc.tile_pool(name="rotated", bufs=8))
        flip_banks = ctx.enter_context(tc.psum_pool(name="flip_banks", bufs=5))
        sum_banks = ctx.enter_context(tc.psum_pool(name="sum_banks", bufs=3))
        ctx.enter_context(tc.manual_schedule())

        x_runs = x.rearrange("b (p t) d -> b p (t d)", t=POS_PER_PART)
        out_runs = [
            out.rearrange("b h (p t) f -> (b h) p (t f)", t=POS_PER_PART) for out in (out_0, out_1)
        ]

        def load_round(r, pieces):
            batch, part = divmod(r, ROUNDS_PER_BATCH)
            rows = row_pool.tile([P, ROUND_TILES * D_IN], BF16)
            width = ROUND_TILES * D_IN // pieces
            for piece in range(pieces):
                start = (part * pieces + piece) * width
                nc.sync.dma_start(
                    out=rows[:, piece * width : (piece + 1) * width],
                    in_=x_runs[batch, :, start : start + width],
                )
            return rows

        def k_onto_partitions(row_words, grouped_words):
            bank = flip_banks.tile([P, WORDS], F32)
            for q in range(WORDS // P):
                nc.tensor.transpose(
                    bank[:, q * P : (q + 1) * P], row_words[:, q * P : (q + 1) * P], identity[:]
                )
            nc.scalar.copy(
                out=grouped_words, in_=bank[:].rearrange("p (g u r) -> p g r u", g=PASSES, u=2)
            )

        position = const.tile([P, POS_PER_PART], I32)
        nc.gpsimd.iota(
            position[:], pattern=[[1, POS_PER_PART]], base=0, channel_multiplier=POS_PER_PART
        )
        partition = const.tile([P, 1], I32)
        nc.gpsimd.iota(partition[:], pattern=[[0, 1]], base=0, channel_multiplier=1)
        identity = const.tile([P, P], F32)
        make_identity(nc, identity[:])

        rows_of = {0: load_round(0, FIRST_LOAD_PIECES)}
        w_rows = const.tile([P, D_IN], BF16)
        nc.sync.dma_start(out=w_rows[:], in_=wqk_w)
        partner_rows = const.tile([P, D_IN], BF16)
        w_halves = wqk_w.rearrange("(n e) k -> e n k", e=2)
        for e in range(2):
            nc.sync.dma_start(out=partner_rows[e:P:2, :], in_=w_halves[1 - e])
        for r in range(1, LOADS_AHEAD):
            rows_of[r] = load_round(r, 1)

        turns = const.tile([P, POS_PER_PART, 2, PAIRS], F32)
        for i in range(PAIRS):
            nc.vector.tensor_scalar(
                out=turns[:, :, 1, i],
                in0=position[:],
                scalar1=turns_per_position(i),
                scalar2=None,
                op0=ALU.mult,
            )
        nc.vector.tensor_scalar(
            out=turns[:, :, 0, :], in0=turns[:, :, 1, :], scalar1=0.25, scalar2=None, op0=ALU.add
        )
        whole_turns = const.tile([P, POS_PER_PART, 2, PAIRS], F32)
        nc.vector.tensor_scalar(
            out=whole_turns[:],
            in0=turns[:],
            scalar1=ROUND_MAGIC,
            scalar2=ROUND_MAGIC,
            op0=ALU.add,
            op1=ALU.subtract,
        )
        part_turns = const.tile([P, POS_PER_PART, 2, PAIRS], F32)
        nc.vector.tensor_tensor(
            out=part_turns[:], in0=turns[:], in1=whole_turns[:], op=ALU.subtract
        )

        w_grouped = const.tile([P, PASSES * TILE_SUMS * 4], BF16, align_bytes=64)
        w_codes = const.tile([P, PASSES * TILE_SUMS], U32, align_bytes=64)
        w_scales = const.tile([P, PASSES * TILE_SUMS], U8, align_bytes=64)

        def prepare_weights():
            odd_partition = const.tile([P, 1], I32)
            nc.vector.tensor_scalar(
                out=odd_partition[:], in0=partition[:], scalar1=1, scalar2=None, op0=ALU.bitwise_and
            )
            sign = const.tile([P, 1], F32)
            nc.vector.tensor_scalar(
                out=sign[:], in0=odd_partition[:], scalar1=2.0, scalar2=-1.0, op0=ALU.mult, op1=ALU.add
            )
            nc.vector.tensor_scalar(
                out=partner_rows[:],
                in0=partner_rows[:],
                scalar1=sign[:, 0:1],
                scalar2=None,
                op0=ALU.mult,
            )
            w_grouped_words = w_grouped[:].bitcast(F32).rearrange(
                "p (g h r u) -> p h g r u", g=PASSES, h=2, u=2
            )
            k_onto_partitions(w_rows[:].bitcast(F32), w_grouped_words[:, 0])
            k_onto_partitions(partner_rows[:].bitcast(F32), w_grouped_words[:, 1])
            nc.vector.quantize_mx(
                out=w_codes[:].bitcast(FP8X4), scales=w_scales[:], in_=w_grouped[:]
            )

        grouped_of, codes_of, scales_of, sums_of, products_of, rotated_of = {}, {}, {}, {}, {}, {}

        def regroup(r):
            grouped = mx_pool.tile([P, ROUND_TILES * D_IN], BF16, align_bytes=64)
            row_words = rows_of[r][:].bitcast(F32)
            grouped_words = grouped[:].bitcast(F32).rearrange(
                "p (j g r u) -> p j g r u", j=ROUND_TILES, g=PASSES, u=2
            )
            for j in range(ROUND_TILES):
                k_onto_partitions(row_words[:, j * WORDS : (j + 1) * WORDS], grouped_words[:, j])
            grouped_of[r] = grouped

        cos_sin = const.tile([P, POS_PER_PART * 2 * PAIRS, 2], F32)
        ROUND_FACTORS = ROUND_TILES * 2 * PAIRS

        def factors_for_round(n):
            these = slice(n * ROUND_FACTORS, (n + 1) * ROUND_FACTORS)
            nc.scalar.activation(
                out=cos_sin[:, these, :],
                in_=part_turns[:]
                .rearrange("p t h i -> p (t h i)")[:, these]
                .unsqueeze(2)
                .to_broadcast([P, ROUND_FACTORS, 2]),
                func=ACT.Sin,
                scale=2.0 * math.pi,
            )

        def quantise(r, half):
            if half == 0:
                codes = mx_pool.tile([P, ROUND_TILES * PASSES * P], U32, align_bytes=64)
                scales = mx_pool.tile([P, ROUND_TILES * PASSES * P], U8, align_bytes=64)
                codes_of[r], scales_of[r] = codes, scales
            words = BANK_TILES * PASSES * P
            nc.vector.quantize_mx(
                out=codes_of[r][:, half * words : (half + 1) * words].bitcast(FP8X4),
                scales=scales_of[r][:, half * words : (half + 1) * words],
                in_=grouped_of[r][:, half * 4 * words : (half + 1) * 4 * words],
            )

        def multiply(r):
            sums_of[r] = []
            for first_tile in range(0, ROUND_TILES, BANK_TILES):
                sums = sum_banks.tile([P, BANK], F32)
                for j in range(BANK_TILES):
                    for g in range(PASSES):
                        at = ((first_tile + j) * PASSES + g) * P
                        nc.tensor.matmul_mx(
                            out=sums[:, j * TILE_SUMS : (j + 1) * TILE_SUMS],
                            lhsT=codes_of[r][:, at : at + P].bitcast(FP8X4),
                            lhsT_scale=scales_of[r][:, at : at + P],
                            rhs=w_codes[:, g * TILE_SUMS : (g + 1) * TILE_SUMS].bitcast(FP8X4),
                            rhs_scale=w_scales[:, g * TILE_SUMS : (g + 1) * TILE_SUMS],
                            start=(g == 0),
                            stop=(g == PASSES - 1),
                        )
                sums_of[r].append(sums)

        def rotate_half(r, half):
            if half == 0:
                products = rope_pool.tile([P, ROUND_TILES * 2, 2, HEAD], F32)
                rotated = out_pool.tile([P, 2, ROUND_TILES, HEAD], F32)
                products_of[r], rotated_of[r] = products, rotated
            bank_rows = BANK_TILES * 2
            first = (r % ROUNDS_PER_BATCH) * ROUND_TILES * 2 + half * bank_rows
            factors = cos_sin[:].rearrange("p (th i) e -> p th (i e)", i=PAIRS)
            nc.vector.tensor_tensor(
                out=products_of[r][:, half * bank_rows : (half + 1) * bank_rows],
                in0=sums_of[r][half][:].rearrange("p (th c f) -> p th c f", c=2, f=HEAD),
                in1=factors[:, first : first + bank_rows]
                .unsqueeze(2)
                .to_broadcast([P, bank_rows, 2, HEAD]),
                op=ALU.mult,
            )
            tiles = slice(half * BANK_TILES, (half + 1) * BANK_TILES)
            by_term = products_of[r][:].rearrange("p (j h) c f -> p h c j f", h=2)
            nc.gpsimd.tensor_tensor(
                out=rotated_of[r][:, :, tiles, :],
                in0=by_term[:, 0, :, tiles, :],
                in1=by_term[:, 1, :, tiles, :],
                op=ALU.add,
            )

        def store(r):
            batch, part = divmod(r, ROUNDS_PER_BATCH)
            run = slice(part * ROUND_TILES * HEAD, (part + 1) * ROUND_TILES * HEAD)
            for c in range(2):
                nc.sync.dma_start(
                    out=out_runs[c][batch, :, run],
                    in_=rotated_of[r][:, c].rearrange("p j f -> p (j f)"),
                )

        regroup(0)
        prepare_weights()
        factors_for_round(0)
        for s in range(1, ROUNDS + 2):
            if s + LOADS_AHEAD - 1 < ROUNDS:
                rows_of[s + LOADS_AHEAD - 1] = load_round(s + LOADS_AHEAD - 1, 1)
            if s < ROUNDS:
                regroup(s)
            if s < ROUNDS_PER_BATCH:
                factors_for_round(s)
            for half in range(ROUND_BANKS):
                if s <= ROUNDS:
                    quantise(s - 1, half)
                if s >= 2:
                    rotate_half(s - 2, half)
            if s <= ROUNDS:
                multiply(s - 1)
            if s >= 2:
                store(s - 2)
